import numpy as np
import ml_dtypes


def mxq(x, axis, fmt="e4m3"):
    dtype, down = {"e4m3": (ml_dtypes.float8_e4m3fn, 7), "e5m2": (ml_dtypes.float8_e5m2, 14)}[fmt]
    v = np.moveaxis(np.asarray(x, np.float32).astype(ml_dtypes.bfloat16).astype(np.float64), axis, -1)
    blocks = v.reshape(v.shape[:-1] + (-1, 32))
    amax = np.abs(blocks).max(-1, keepdims=True)
    byte = np.maximum(np.where(amax > 0, np.frexp(amax)[1] - 1 + 127, 0) - down, 1)
    scale = np.exp2(byte - 127.0)
    codes = (blocks / scale).astype(np.float32).astype(dtype).astype(np.float64)
    return np.moveaxis((codes * scale).reshape(v.shape), -1, axis)


WIDE = False


def mx_kscale(k):
    if not WIDE:
        return np.ones(k)
    levels = np.array([10, -10, 5, -5, 0])
    a = np.random.permutation(np.resize(levels, k // 512 * 4)).reshape(k // 512, 4)
    idx = np.arange(k)
    return np.exp2(a[idx // 512, idx % 128 // 32])


BF16 = ml_dtypes.bfloat16


def bf(x):
    return np.asarray(x, np.float32).astype(BF16)


def f64(x):
    return np.asarray(x).astype(np.float64)


B, I, H, AH, AI, G = 128, 128, 384, 256, 128, 4
EPS = 1e-5
K = I + H


def sigmoid(v):
    return 1.0 / (1.0 + np.exp(-v))


def ln(v, w, b):
    mu = v.mean(-1, keepdims=True)
    var = ((v - mu) ** 2).mean(-1, keepdims=True)
    return (v - mu) / np.sqrt(var + EPS) * w + b


def setup_inputs():
    n = np.random.standard_normal
    s = mx_kscale(K)
    return {
        "x": bf(n((B, I)) * s[:I]),
        "hx": bf(n((B, H)) * s[I:]),
        "ah": bf(n((B, AH))),
        "ac": bf(n((B, AH))),
        "a_w_ih": bf(n((G * AH, K)) / np.sqrt(K) / s),
        "a_w_hh": bf(n((G * AH, AH)) / np.sqrt(AH)),
        "a_ln_i_w": bf(1.0 + 0.1 * n(G * AH)),
        "a_ln_i_b": bf(0.2 * n(G * AH)),
        "a_ln_h_w": bf(1.0 + 0.1 * n(G * AH)),
        "a_ln_h_b": bf(0.2 * n(G * AH)),
        "a_ln_c_w": bf(1.0 + 0.1 * n(AH)),
        "a_ln_c_b": bf(0.2 * n(AH)),
    }


def reference(x, hx, ah, ac, a_w_ih, a_w_hh, a_ln_i_w, a_ln_i_b, a_ln_h_w, a_ln_h_b, a_ln_c_w, a_ln_c_b):
    ai = np.concatenate([f64(x), f64(hx)], axis=1)
    ig = ln(mxq(ai, 1, "e4m3") @ mxq(f64(a_w_ih), 1, "e4m3").T, f64(a_ln_i_w), f64(a_ln_i_b))
    hg = ln(f64(ah) @ f64(a_w_hh).T, f64(a_ln_h_w), f64(a_ln_h_b))
    g = ig + hg
    gi, gf, gj, go = np.split(g, G, axis=1)
    acy = ln(sigmoid(gf) * f64(ac) + sigmoid(gi) * np.tanh(gj), f64(a_ln_c_w), f64(a_ln_c_b))
    ada = sigmoid(go) * np.tanh(acy)
    return ada, acy

@@ -1,0 +1,319 @@
+from contextlib import ExitStack
+
+import concourse.mybir as mybir
+from concourse.masks import make_identity
+
+F32 = mybir.dt.float32
+BF16 = mybir.dt.bfloat16
+U32 = mybir.dt.uint32
+U8 = mybir.dt.uint8
+FP8X4 = mybir.dt.float8_e4m3fn_x4
+ALU = mybir.AluOpType
+ACT = mybir.ActivationFunctionType
+
+P = 128
+X_FEATURES = 128
+K_IH = 512
+K_HH = 256
+CELL = 256
+GATES = 4
+N = GATES * CELL
+BANK = 512
+HALVES = N // BANK
+EPS = 1e-5
+
+FLOPS = 2 * P * N * (K_IH + K_HH)
+
+
+def tile_adaptivelstmcell_pa_s_kernel(
+    tc,
+    x,
+    hx,
+    ah,
+    ac,
+    a_w_ih,
+    a_w_hh,
+    a_ln_i_w,
+    a_ln_i_b,
+    a_ln_h_w,
+    a_ln_h_b,
+    a_ln_c_w,
+    a_ln_c_b,
+    out_0,
+    out_1,
+):
+    nc = tc.nc
+    with ExitStack() as ctx:
+        keep = ctx.enter_context(tc.tile_pool(name="keep", bufs=1))
+        banks = ctx.enter_context(tc.psum_pool(name="banks", bufs=4))
+        sums = ctx.enter_context(tc.psum_pool(name="sums", bufs=1))
+
+        ident_f32 = keep.tile([P, P], F32)
+        make_identity(nc, ident_f32[:])
+        ident_bf16 = keep.tile([P, P], BF16)
+        make_identity(nc, ident_bf16[:])
+        minus_half = keep.tile([P, 1], F32)
+        nc.vector.memset(minus_half[:], -0.5)
+        warm_in = keep.tile([P, 1], F32)
+        warm_out = keep.tile([P, 1], F32)
+        nc.vector.memset(warm_in[:], 0.0)
+        nc.scalar.activation(out=warm_out[:], in_=warm_in[:], func=ACT.Sigmoid)
+
+        ai_sb = keep.tile([P, K_IH], BF16)
+        nc.sync.dma_start(out=ai_sb[:, 0:X_FEATURES], in_=x)
+        nc.sync.dma_start(out=ai_sb[:, X_FEATURES:K_IH], in_=hx)
+
+        wih_sb = keep.tile([P, GATES, 2 * K_IH], BF16)
+        wih_rows = a_w_ih.rearrange("(g p r) k -> g p (r k)", g=GATES, p=P, r=2)
+        nc.sync.dma_start(out=wih_sb[:, 0, :], in_=wih_rows[0])
+        nc.sync.dma_start(out=wih_sb[:, 1, :], in_=wih_rows[1])
+
+        ln_rows = keep.tile([P, CELL], BF16)
+        nc.vector.memset(ln_rows[:], 0.0)
+        ROW_I_W, ROW_I_B, ROW_H_B, ROW_H_W = 0, 4, 8, 12
+        for first_row, vector in (
+            (ROW_I_W, a_ln_i_w),
+            (ROW_I_B, a_ln_i_b),
+            (ROW_H_B, a_ln_h_b),
+            (ROW_H_W, a_ln_h_w),
+        ):
+            nc.sync.dma_start(
+                out=ln_rows[first_row : first_row + GATES, :],
+                in_=vector.rearrange("(r c) -> r c", c=CELL),
+            )
+        nc.sync.dma_start(out=wih_sb[:, 2, :], in_=wih_rows[2])
+        nc.sync.dma_start(out=wih_sb[:, 3, :], in_=wih_rows[3])
+
+        ah_sb = keep.tile([P, K_HH], BF16)
+        nc.sync.dma_start(out=ah_sb[:], in_=ah)
+        whh_sb = keep.tile([P, N // P, K_HH], BF16)
+        whh_rows = a_w_hh.rearrange("(c p) k -> p c k", p=P)
+        for half in range(HALVES):
+            blocks = slice(4 * half, 4 * half + 4)
+            nc.sync.dma_start(out=whh_sb[:, blocks, :], in_=whh_rows[:, blocks, :])
+
+        lnc_rows = keep.tile([P, CELL], BF16)
+        nc.vector.memset(lnc_rows[:], 0.0)
+        nc.sync.dma_start(out=lnc_rows[0:1, :], in_=a_ln_c_w.rearrange("(r c) -> r c", c=CELL))
+        nc.sync.dma_start(out=lnc_rows[1:2, :], in_=a_ln_c_b.rearrange("(r c) -> r c", c=CELL))
+        ac_sb = keep.tile([P, CELL], BF16)
+        nc.sync.dma_start(out=ac_sb[:], in_=ac)
+
+        def rows_to_columns(rows, count, name):
+            bank = banks.tile([P, P], F32, tag="bank", name=name + "_ps")
+            nc.tensor.transpose(bank[:], rows[:].bitcast(F32), ident_f32[:])
+            columns = keep.tile([P, count], F32, name=name)
+            nc.vector.tensor_copy(out=columns[:], in_=bank[:, 0:count])
+            return columns
+
+        def spread(columns, first, count, name):
+            bank = banks.tile([P, count * P], F32, tag="bank", name=name)
+            for i in range(count):
+                nc.tensor.transpose(
+                    bank[:, i * P : (i + 1) * P],
+                    columns[:, first + i : first + i + 1].to_broadcast([P, P]),
+                    ident_f32[:],
+                )
+            return bank
+
+        def inverse_std(mean_var, name):
+            shifted = keep.tile([P, 1], F32, name=name + "_var_eps")
+            nc.vector.tensor_scalar_add(out=shifted[:], in0=mean_var[:, 1:2], scalar1=EPS)
+            rstd = keep.tile([P, 1], F32, name=name)
+            nc.gpsimd.tensor_tensor(out=rstd[:], in0=shifted[:], in1=minus_half[:], op=ALU.pow)
+            return rstd
+
+        ai_bank = banks.tile([P, 2, P], F32, tag="bank")
+        for u in range(2):
+            nc.tensor.transpose(
+                ai_bank[:, u, :], ai_sb[:].bitcast(F32)[:, u * P : (u + 1) * P], ident_f32[:]
+            )
+        ai_grouped = keep.tile([P, P, 2], F32, align_bytes=64)
+        nc.vector.tensor_copy(out=ai_grouped[:], in_=ai_bank[:].rearrange("p u b -> p b u"))
+        ai_codes = keep.tile([P, P], U32, align_bytes=64)
+        ai_scales = keep.tile([P, P], U8, align_bytes=64)
+        nc.vector.quantize_mx(
+            out=ai_codes[:].bitcast(FP8X4),
+            scales=ai_scales[:],
+            in_=ai_grouped[:].rearrange("p b u -> p (b u)").bitcast(BF16),
+        )
+
+        w_grouped = keep.tile([P, GATES, 2 * CELL], F32, align_bytes=64)
+        w_codes = keep.tile([P, N], U32, align_bytes=64)
+        w_scales = keep.tile([P, N], U8, align_bytes=64)
+        for g in range(GATES):
+            w_bank = banks.tile([P, 4, P], F32, tag="bank")
+            words = wih_sb[:, g, :].bitcast(F32)
+            for ru in range(4):
+                nc.tensor.transpose(w_bank[:, ru, :], words[:, ru * P : (ru + 1) * P], ident_f32[:])
+            copy_out = nc.scalar.copy if g % 2 == 0 else nc.vector.tensor_copy
+            copy_out(
+                out=w_grouped[:, g, :].rearrange("p (j r u) -> p j r u", r=2, u=2),
+                in_=w_bank[:].rearrange("p (r u) j -> p j r u", r=2, u=2),
+            )
+            gate_cols = slice(g * CELL, (g + 1) * CELL)
+            nc.vector.quantize_mx(
+                out=w_codes[:, gate_cols].bitcast(FP8X4),
+                scales=w_scales[:, gate_cols],
+                in_=w_grouped[:, g, :].bitcast(BF16),
+            )
+
+        ln_columns = rows_to_columns(ln_rows, 4 * GATES, "ln_columns")
+        gain_i = keep.tile([P, BANK], F32)
+        nc.scalar.copy(out=gain_i[:], in_=spread(ln_columns, ROW_I_W, GATES, "gain_i_ps")[:])
+        shift_i = keep.tile([P, BANK], F32)
+        nc.scalar.copy(out=shift_i[:], in_=spread(ln_columns, ROW_I_B, GATES, "shift_i_ps")[:])
+        shift_sum = keep.tile([P, N], F32)
+        nc.vector.tensor_tensor(
+            out=shift_sum[:],
+            in0=spread(ln_columns, ROW_H_B, GATES, "shift_h_ps")[:].bitcast(BF16),
+            in1=shift_i[:].bitcast(BF16),
+            op=ALU.add,
+        )
+        gain_h = keep.tile([P, BANK], F32)
+        nc.scalar.copy(out=gain_h[:], in_=spread(ln_columns, ROW_H_W, GATES, "gain_h_ps")[:])
+
+        vi = [sums.tile([P, BANK], F32, name="vi%d" % half) for half in range(HALVES)]
+        stats_i = keep.tile([P, HALVES, 6], F32)
+        for half in range(HALVES):
+            cols = slice(half * BANK, (half + 1) * BANK)
+            nc.tensor.matmul_mx(
+                out=vi[half][:],
+                lhsT=ai_codes[:].bitcast(FP8X4),
+                lhsT_scale=ai_scales[:],
+                rhs=w_codes[:, cols].bitcast(FP8X4),
+                rhs_scale=w_scales[:, cols],
+                start=True,
+                stop=True,
+            )
+            nc.vector.bn_stats(out=stats_i[:, half, :], in_=vi[half][:])
+        mean_var_i = keep.tile([P, 2], F32)
+        nc.vector.bn_aggr(out=mean_var_i[:], in_=stats_i[:].rearrange("p c s -> p (c s)"))
+        rstd_i = inverse_std(mean_var_i, "rstd_i")
+        centred_i = keep.tile([P, N], F32)
+        for half in range(HALVES):
+            cols = slice(half * BANK, (half + 1) * BANK)
+            nc.vector.scalar_tensor_tensor(
+                out=centred_i[:, cols],
+                in0=vi[half][:],
+                scalar=mean_var_i[:, 0:1],
+                in1=gain_i[:].bitcast(BF16)[:, cols],
+                op0=ALU.subtract,
+                op1=ALU.mult,
+            )
+        i_part = keep.tile([P, N], F32)
+        nc.vector.scalar_tensor_tensor(
+            out=i_part[:],
+            in0=centred_i[:],
+            scalar=rstd_i[:],
+            in1=shift_sum[:],
+            op0=ALU.mult,
+            op1=ALU.add,
+        )
+
+        ah_bank = banks.tile([P, 2, P], BF16, tag="bank")
+        for kc in range(2):
+            nc.tensor.transpose(ah_bank[:, kc, :], ah_sb[:, kc * P : (kc + 1) * P], ident_bf16[:])
+        ahT = keep.tile([P, 2, P], BF16)
+        nc.scalar.copy(out=ahT[:], in_=ah_bank[:])
+        whhT = keep.tile([P, HALVES, 2, BANK], BF16)
+        vh = [sums.tile([P, BANK], F32, name="vh%d" % half) for half in range(HALVES)]
+        stats_h = keep.tile([P, HALVES, 6], F32)
+        for half in range(HALVES):
+            whh_bank = banks.tile([P, 2, 4, P], BF16, tag="bank")
+            for kc in range(2):
+                for c in range(4):
+                    nc.tensor.transpose(
+                        whh_bank[:, kc, c, :],
+                        whh_sb[:, 4 * half + c, kc * P : (kc + 1) * P],
+                        ident_bf16[:],
+                    )
+            nc.scalar.copy(
+                out=whhT[:, half, :, :], in_=whh_bank[:].rearrange("p k c j -> p k (c j)")
+            )
+            for kc in range(2):
+                nc.tensor.matmul(
+                    out=vh[half][:],
+                    lhsT=ahT[:, kc, :],
+                    rhs=whhT[:, half, kc, :],
+                    start=(kc == 0),
+                    stop=(kc == 1),
+                )
+            nc.vector.bn_stats(out=stats_h[:, half, :], in_=vh[half][:])
+        mean_var_h = keep.tile([P, 2], F32)
+        nc.vector.bn_aggr(out=mean_var_h[:], in_=stats_h[:].rearrange("p c s -> p (c s)"))
+        rstd_h = inverse_std(mean_var_h, "rstd_h")
+
+        lnc_columns = rows_to_columns(lnc_rows, 2, "lnc_columns")
+        gain_shift_c = keep.tile([P, CELL], F32)
+        nc.scalar.copy(out=gain_shift_c[:], in_=spread(lnc_columns, 0, 2, "gain_shift_c_ps")[:])
+        gain_c = gain_shift_c[:].bitcast(BF16)[:, 0:CELL]
+        shift_c = gain_shift_c[:].bitcast(BF16)[:, CELL : 2 * CELL]
+
+        centred_h = keep.tile([P, N], F32)
+        g_sum = keep.tile([P, N], F32)
+        gate = keep.tile([P, N], F32)
+        for first, width, func in (
+            (0, 2 * CELL, ACT.Sigmoid),
+            (2 * CELL, CELL, ACT.Tanh),
+            (3 * CELL, CELL, ACT.Sigmoid),
+        ):
+            cols = slice(first, first + width)
+            nc.vector.scalar_tensor_tensor(
+                out=centred_h[:, cols],
+                in0=vh[first // BANK][:, first % BANK : first % BANK + width],
+                scalar=mean_var_h[:, 0:1],
+                in1=gain_h[:].bitcast(BF16)[:, cols],
+                op0=ALU.subtract,
+                op1=ALU.mult,
+            )
+            nc.vector.scalar_tensor_tensor(
+                out=g_sum[:, cols],
+                in0=centred_h[:, cols],
+                scalar=rstd_h[:],
+                in1=i_part[:, cols],
+                op0=ALU.mult,
+                op1=ALU.add,
+            )
+            nc.scalar.activation(out=gate[:, cols], in_=g_sum[:, cols], func=func)
+        gate_in = gate[:, 0:CELL]
+        gate_forget = gate[:, CELL : 2 * CELL]
+        gate_cell = gate[:, 2 * CELL : 3 * CELL]
+        gate_out = gate[:, 3 * CELL : 4 * CELL]
+
+        kept = keep.tile([P, CELL], F32)
+        nc.vector.tensor_mul(out=kept[:], in0=gate_forget, in1=ac_sb[:])
+        fresh = keep.tile([P, CELL], F32)
+        nc.vector.tensor_mul(out=fresh[:], in0=gate_in, in1=gate_cell)
+        cell = keep.tile([P, CELL], F32)
+        nc.vector.tensor_add(out=cell[:], in0=kept[:], in1=fresh[:])
+        stats_c = keep.tile([P, 6], F32)
+        nc.vector.bn_stats(out=stats_c[:], in_=cell[:])
+        mean_var_c = keep.tile([P, 2], F32)
+        nc.vector.bn_aggr(out=mean_var_c[:], in_=stats_c[:])
+        rstd_c = inverse_std(mean_var_c, "rstd_c")
+        centred_c = keep.tile([P, CELL], F32)
+        nc.vector.scalar_tensor_tensor(
+            out=centred_c[:],
+            in0=cell[:],
+            scalar=mean_var_c[:, 0:1],
+            in1=gain_c,
+            op0=ALU.subtract,
+            op1=ALU.mult,
+        )
+        acy = keep.tile([P, CELL], F32)
+        nc.vector.scalar_tensor_tensor(
+            out=acy[:],
+            in0=centred_c[:],
+            scalar=rstd_c[:],
+            in1=shift_c,
+            op0=ALU.mult,
+            op1=ALU.add,
+        )
+        nc.sync.dma_start(out=out_1, in_=acy[:])
+
+        tanh_acy = keep.tile([P, CELL], F32)
+        nc.scalar.activation(out=tanh_acy[:], in_=acy[:], func=ACT.Tanh)
+        ada = keep.tile([P, CELL], F32)
+        nc.vector.tensor_mul(out=ada[:], in0=gate_out, in1=tanh_acy[:])
+        nc.sync.dma_start(out=out_0, in_=ada[:])

@@ -50,8 +50,6 @@ def tile_adaptivelstmcell_pa_s_kernel(
 
         ident_f32 = keep.tile([P, P], F32)
         make_identity(nc, ident_f32[:])
-        ident_bf16 = keep.tile([P, P], BF16)
-        make_identity(nc, ident_bf16[:])
         minus_half = keep.tile([P, 1], F32)
         nc.vector.memset(minus_half[:], -0.5)
         warm_in = keep.tile([P, 1], F32)
@@ -59,56 +57,47 @@ def tile_adaptivelstmcell_pa_s_kernel(
         nc.vector.memset(warm_in[:], 0.0)
         nc.scalar.activation(out=warm_out[:], in_=warm_in[:], func=ACT.Sigmoid)
 
-        ai_sb = keep.tile([P, K_IH], BF16)
-        nc.sync.dma_start(out=ai_sb[:, 0:X_FEATURES], in_=x)
-        nc.sync.dma_start(out=ai_sb[:, X_FEATURES:K_IH], in_=hx)
-
-        wih_sb = keep.tile([P, GATES, 2 * K_IH], BF16)
-        wih_rows = a_w_ih.rearrange("(g p r) k -> g p (r k)", g=GATES, p=P, r=2)
-        nc.sync.dma_start(out=wih_sb[:, 0, :], in_=wih_rows[0])
-        nc.sync.dma_start(out=wih_sb[:, 1, :], in_=wih_rows[1])
+        ah_sb = keep.tile([P, K_HH], BF16)
+        nc.sync.dma_start(out=ah_sb[:], in_=ah)
+        whh_sb = keep.tile([P, GATES, 2 * K_HH], BF16)
+        whh_rows = a_w_hh.rearrange("(g p r) k -> p g (r k)", g=GATES, p=P, r=2)
+        for pair in range(HALVES):
+            gates = slice(2 * pair, 2 * pair + 2)
+            nc.sync.dma_start(out=whh_sb[:, gates, :], in_=whh_rows[:, gates, :])
 
         ln_rows = keep.tile([P, CELL], BF16)
         nc.vector.memset(ln_rows[:], 0.0)
-        ROW_I_W, ROW_I_B, ROW_H_B, ROW_H_W = 0, 4, 8, 12
+        ROW_SHIFT_I, ROW_SHIFT_H, ROW_GAIN_H, LN_ROWS = 0, 4, 8, 12
         for first_row, vector in (
-            (ROW_I_W, a_ln_i_w),
-            (ROW_I_B, a_ln_i_b),
-            (ROW_H_B, a_ln_h_b),
-            (ROW_H_W, a_ln_h_w),
+            (ROW_SHIFT_I, a_ln_i_b),
+            (ROW_SHIFT_H, a_ln_h_b),
+            (ROW_GAIN_H, a_ln_h_w),
         ):
             nc.sync.dma_start(
                 out=ln_rows[first_row : first_row + GATES, :],
                 in_=vector.rearrange("(r c) -> r c", c=CELL),
             )
-        nc.sync.dma_start(out=wih_sb[:, 2, :], in_=wih_rows[2])
-        nc.sync.dma_start(out=wih_sb[:, 3, :], in_=wih_rows[3])
 
-        ah_sb = keep.tile([P, K_HH], BF16)
-        nc.sync.dma_start(out=ah_sb[:], in_=ah)
-        whh_sb = keep.tile([P, N // P, K_HH], BF16)
-        whh_rows = a_w_hh.rearrange("(c p) k -> p c k", p=P)
-        for half in range(HALVES):
-            blocks = slice(4 * half, 4 * half + 4)
-            nc.sync.dma_start(out=whh_sb[:, blocks, :], in_=whh_rows[:, blocks, :])
+        ai_sb = keep.tile([P, K_IH], BF16)
+        nc.sync.dma_start(out=ai_sb[:, 0:X_FEATURES], in_=x)
+        nc.sync.dma_start(out=ai_sb[:, X_FEATURES:K_IH], in_=hx)
+        wih_sb = keep.tile([P, GATES, 2 * K_IH], BF16)
+        wih_rows = a_w_ih.rearrange("(g p r) k -> p g (r k)", g=GATES, p=P, r=2)
+        for g in range(GATES):
+            nc.sync.dma_start(out=wih_sb[:, g, :], in_=wih_rows[:, g, :])
 
-        lnc_rows = keep.tile([P, CELL], BF16)
-        nc.vector.memset(lnc_rows[:], 0.0)
-        nc.sync.dma_start(out=lnc_rows[0:1, :], in_=a_ln_c_w.rearrange("(r c) -> r c", c=CELL))
-        nc.sync.dma_start(out=lnc_rows[1:2, :], in_=a_ln_c_b.rearrange("(r c) -> r c", c=CELL))
         ac_sb = keep.tile([P, CELL], BF16)
         nc.sync.dma_start(out=ac_sb[:], in_=ac)
+        gain_i = keep.tile([P, N], BF16)
+        nc.sync.dma_start(out=gain_i[:], in_=a_ln_i_w.partition_broadcast(P))
+        gain_c = keep.tile([P, CELL], BF16)
+        nc.sync.dma_start(out=gain_c[:], in_=a_ln_c_w.partition_broadcast(P))
+        shift_c = keep.tile([P, CELL], BF16)
+        nc.sync.dma_start(out=shift_c[:], in_=a_ln_c_b.partition_broadcast(P))
 
-        def rows_to_columns(rows, count, name):
-            bank = banks.tile([P, P], F32, tag="bank", name=name + "_ps")
-            nc.tensor.transpose(bank[:], rows[:].bitcast(F32), ident_f32[:])
-            columns = keep.tile([P, count], F32, name=name)
-            nc.vector.tensor_copy(out=columns[:], in_=bank[:, 0:count])
-            return columns
-
-        def spread(columns, first, count, name):
-            bank = banks.tile([P, count * P], F32, tag="bank", name=name)
-            for i in range(count):
+        def spread(columns, first, name):
+            bank = banks.tile([P, 4 * P], F32, tag="bank", name=name)
+            for i in range(4):
                 nc.tensor.transpose(
                     bank[:, i * P : (i + 1) * P],
                     columns[:, first + i : first + i + 1].to_broadcast([P, P]),
@@ -123,13 +112,98 @@ def tile_adaptivelstmcell_pa_s_kernel(
             nc.gpsimd.tensor_tensor(out=rstd[:], in0=shifted[:], in1=minus_half[:], op=ALU.pow)
             return rstd
 
+        ah_bank = banks.tile([P, P], F32, tag="bank")
+        nc.tensor.transpose(ah_bank[:], ah_sb[:].bitcast(F32), ident_f32[:])
+        ahT = keep.tile([P, 2, P], BF16)
+        nc.vector.tensor_copy(
+            out=ahT[:], in_=ah_bank[:].bitcast(BF16).rearrange("p (b e) -> p e b", e=2)
+        )
+        whhT = keep.tile([P, N], F32)
+        for pair in range(HALVES):
+            whh_bank = banks.tile([P, 4, P], F32, tag="bank")
+            for gr in range(4):
+                words = whh_sb[:, 2 * pair + gr // 2, :].bitcast(F32)
+                nc.tensor.transpose(
+                    whh_bank[:, gr, :], words[:, (gr % 2) * P : (gr % 2 + 1) * P], ident_f32[:]
+                )
+            nc.vector.tensor_copy(
+                out=whhT[:, pair * BANK : (pair + 1) * BANK].rearrange(
+                    "p (g j r) -> p g j r", g=2, r=2
+                ),
+                in_=whh_bank[:].rearrange("p (g r) j -> p g j r", g=2, r=2),
+            )
+
+        ln_bank = banks.tile([P, P], F32, tag="bank")
+        nc.tensor.transpose(ln_bank[:], ln_rows[:].bitcast(F32), ident_f32[:])
+        ln_columns = keep.tile([P, LN_ROWS], F32)
+        nc.vector.tensor_copy(out=ln_columns[:], in_=ln_bank[:, 0:LN_ROWS])
+        ln_values = ln_columns[:].bitcast(BF16)
+        shift_columns = keep.tile([P, 2 * GATES], F32)
+        nc.vector.tensor_tensor(
+            out=shift_columns[:],
+            in0=ln_values[:, 2 * ROW_SHIFT_I : 2 * ROW_SHIFT_I + 2 * GATES],
+            in1=ln_values[:, 2 * ROW_SHIFT_H : 2 * ROW_SHIFT_H + 2 * GATES],
+            op=ALU.add,
+        )
+
+        whhT_values = whhT[:].bitcast(BF16).rearrange("p (n e) -> p n e", e=2)
+        vh = [sums.tile([P, BANK], F32, name="vh%d" % half) for half in range(HALVES)]
+        stats_h = keep.tile([P, HALVES, 6], F32)
+        for half in range(HALVES):
+            for e in range(2):
+                nc.tensor.matmul(
+                    out=vh[half][:],
+                    lhsT=ahT[:, e, :],
+                    rhs=whhT_values[:, half * BANK : (half + 1) * BANK, e],
+                    start=(e == 0),
+                    stop=(e == 1),
+                )
+            nc.vector.bn_stats(out=stats_h[:, half, :], in_=vh[half][:])
+        mean_var_h = keep.tile([P, 2], F32)
+        nc.vector.bn_aggr(out=mean_var_h[:], in_=stats_h[:].rearrange("p c s -> p (c s)"))
+        rstd_h = inverse_std(mean_var_h, "rstd_h")
+
+        gain_h = keep.tile([P, BANK], F32)
+        nc.scalar.copy(out=gain_h[:], in_=spread(ln_columns, ROW_GAIN_H, "gain_h_ps")[:])
+        shift_sum = keep.tile([P, N], F32)
+        for half in range(HALVES):
+            nc.scalar.copy(
+                out=shift_sum[:, half * BANK : (half + 1) * BANK].rearrange(
+                    "p (r w e) -> p r w e", r=2, e=2
+                ),
+                in_=spread(shift_columns, 4 * half, "shift_ps%d" % half)[:].rearrange(
+                    "p (r e w) -> p r w e", r=2, e=2
+                ),
+            )
+
+        centred_h = keep.tile([P, N], F32)
+        for half in range(HALVES):
+            cols = slice(half * BANK, (half + 1) * BANK)
+            nc.vector.scalar_tensor_tensor(
+                out=centred_h[:, cols],
+                in0=vh[half][:],
+                scalar=mean_var_h[:, 0:1],
+                in1=gain_h[:].bitcast(BF16)[:, cols],
+                op0=ALU.subtract,
+                op1=ALU.mult,
+            )
+        h_part = keep.tile([P, N], F32)
+        nc.vector.scalar_tensor_tensor(
+            out=h_part[:],
+            in0=centred_h[:],
+            scalar=rstd_h[:],
+            in1=shift_sum[:],
+            op0=ALU.mult,
+            op1=ALU.add,
+        )
+
         ai_bank = banks.tile([P, 2, P], F32, tag="bank")
         for u in range(2):
             nc.tensor.transpose(
                 ai_bank[:, u, :], ai_sb[:].bitcast(F32)[:, u * P : (u + 1) * P], ident_f32[:]
             )
         ai_grouped = keep.tile([P, P, 2], F32, align_bytes=64)
-        nc.vector.tensor_copy(out=ai_grouped[:], in_=ai_bank[:].rearrange("p u b -> p b u"))
+        nc.scalar.copy(out=ai_grouped[:], in_=ai_bank[:].rearrange("p u b -> p b u"))
         ai_codes = keep.tile([P, P], U32, align_bytes=64)
         ai_scales = keep.tile([P, P], U8, align_bytes=64)
         nc.vector.quantize_mx(
@@ -146,8 +220,7 @@ def tile_adaptivelstmcell_pa_s_kernel(
             words = wih_sb[:, g, :].bitcast(F32)
             for ru in range(4):
                 nc.tensor.transpose(w_bank[:, ru, :], words[:, ru * P : (ru + 1) * P], ident_f32[:])
-            copy_out = nc.scalar.copy if g % 2 == 0 else nc.vector.tensor_copy
-            copy_out(
+            nc.scalar.copy(
                 out=w_grouped[:, g, :].rearrange("p (j r u) -> p j r u", r=2, u=2),
                 in_=w_bank[:].rearrange("p (r u) j -> p j r u", r=2, u=2),
             )
@@ -158,131 +231,65 @@ def tile_adaptivelstmcell_pa_s_kernel(
                 in_=w_grouped[:, g, :].bitcast(BF16),
             )
 
-        ln_columns = rows_to_columns(ln_rows, 4 * GATES, "ln_columns")
-        gain_i = keep.tile([P, BANK], F32)
-        nc.scalar.copy(out=gain_i[:], in_=spread(ln_columns, ROW_I_W, GATES, "gain_i_ps")[:])
-        shift_i = keep.tile([P, BANK], F32)
-        nc.scalar.copy(out=shift_i[:], in_=spread(ln_columns, ROW_I_B, GATES, "shift_i_ps")[:])
-        shift_sum = keep.tile([P, N], F32)
-        nc.vector.tensor_tensor(
-            out=shift_sum[:],
-            in0=spread(ln_columns, ROW_H_B, GATES, "shift_h_ps")[:].bitcast(BF16),
-            in1=shift_i[:].bitcast(BF16),
-            op=ALU.add,
-        )
-        gain_h = keep.tile([P, BANK], F32)
-        nc.scalar.copy(out=gain_h[:], in_=spread(ln_columns, ROW_H_W, GATES, "gain_h_ps")[:])
-
         vi = [sums.tile([P, BANK], F32, name="vi%d" % half) for half in range(HALVES)]
-        stats_i = keep.tile([P, HALVES, 6], F32)
-        for half in range(HALVES):
-            cols = slice(half * BANK, (half + 1) * BANK)
+        stats_i = keep.tile([P, GATES, 6], F32)
+        for g in range(GATES):
+            gate_cols = slice(g * CELL, (g + 1) * CELL)
+            vi_gate = vi[g // 2][:, (g % 2) * CELL : (g % 2 + 1) * CELL]
             nc.tensor.matmul_mx(
-                out=vi[half][:],
+                out=vi_gate,
                 lhsT=ai_codes[:].bitcast(FP8X4),
                 lhsT_scale=ai_scales[:],
-                rhs=w_codes[:, cols].bitcast(FP8X4),
-                rhs_scale=w_scales[:, cols],
+                rhs=w_codes[:, gate_cols].bitcast(FP8X4),
+                rhs_scale=w_scales[:, gate_cols],
                 start=True,
                 stop=True,
             )
-            nc.vector.bn_stats(out=stats_i[:, half, :], in_=vi[half][:])
+            nc.vector.bn_stats(out=stats_i[:, g, :], in_=vi_gate)
         mean_var_i = keep.tile([P, 2], F32)
         nc.vector.bn_aggr(out=mean_var_i[:], in_=stats_i[:].rearrange("p c s -> p (c s)"))
         rstd_i = inverse_std(mean_var_i, "rstd_i")
+
         centred_i = keep.tile([P, N], F32)
-        for half in range(HALVES):
-            cols = slice(half * BANK, (half + 1) * BANK)
-            nc.vector.scalar_tensor_tensor(
-                out=centred_i[:, cols],
-                in0=vi[half][:],
-                scalar=mean_var_i[:, 0:1],
-                in1=gain_i[:].bitcast(BF16)[:, cols],
-                op0=ALU.subtract,
-                op1=ALU.mult,
-            )
-        i_part = keep.tile([P, N], F32)
-        nc.vector.scalar_tensor_tensor(
-            out=i_part[:],
-            in0=centred_i[:],
-            scalar=rstd_i[:],
-            in1=shift_sum[:],
-            op0=ALU.mult,
-            op1=ALU.add,
-        )
-
-        ah_bank = banks.tile([P, 2, P], BF16, tag="bank")
-        for kc in range(2):
-            nc.tensor.transpose(ah_bank[:, kc, :], ah_sb[:, kc * P : (kc + 1) * P], ident_bf16[:])
-        ahT = keep.tile([P, 2, P], BF16)
-        nc.scalar.copy(out=ahT[:], in_=ah_bank[:])
-        whhT = keep.tile([P, HALVES, 2, BANK], BF16)
-        vh = [sums.tile([P, BANK], F32, name="vh%d" % half) for half in range(HALVES)]
-        stats_h = keep.tile([P, HALVES, 6], F32)
-        for half in range(HALVES):
-            whh_bank = banks.tile([P, 2, 4, P], BF16, tag="bank")
-            for kc in range(2):
-                for c in range(4):
-                    nc.tensor.transpose(
-                        whh_bank[:, kc, c, :],
-                        whh_sb[:, 4 * half + c, kc * P : (kc + 1) * P],
-                        ident_bf16[:],
-                    )
-            nc.scalar.copy(
-                out=whhT[:, half, :, :], in_=whh_bank[:].rearrange("p k c j -> p k (c j)")
-            )
-            for kc in range(2):
-                nc.tensor.matmul(
-                    out=vh[half][:],
-                    lhsT=ahT[:, kc, :],
-                    rhs=whhT[:, half, kc, :],
-                    start=(kc == 0),
-                    stop=(kc == 1),
-                )
-            nc.vector.bn_stats(out=stats_h[:, half, :], in_=vh[half][:])
-        mean_var_h = keep.tile([P, 2], F32)
-        nc.vector.bn_aggr(out=mean_var_h[:], in_=stats_h[:].rearrange("p c s -> p (c s)"))
-        rstd_h = inverse_std(mean_var_h, "rstd_h")
-
-        lnc_columns = rows_to_columns(lnc_rows, 2, "lnc_columns")
-        gain_shift_c = keep.tile([P, CELL], F32)
-        nc.scalar.copy(out=gain_shift_c[:], in_=spread(lnc_columns, 0, 2, "gain_shift_c_ps")[:])
-        gain_c = gain_shift_c[:].bitcast(BF16)[:, 0:CELL]
-        shift_c = gain_shift_c[:].bitcast(BF16)[:, CELL : 2 * CELL]
-
-        centred_h = keep.tile([P, N], F32)
         g_sum = keep.tile([P, N], F32)
         gate = keep.tile([P, N], F32)
-        for first, width, func in (
-            (0, 2 * CELL, ACT.Sigmoid),
-            (2 * CELL, CELL, ACT.Tanh),
-            (3 * CELL, CELL, ACT.Sigmoid),
-        ):
-            cols = slice(first, first + width)
+
+        def centre(first, width):
             nc.vector.scalar_tensor_tensor(
-                out=centred_h[:, cols],
-                in0=vh[first // BANK][:, first % BANK : first % BANK + width],
-                scalar=mean_var_h[:, 0:1],
-                in1=gain_h[:].bitcast(BF16)[:, cols],
+                out=centred_i[:, first : first + width],
+                in0=vi[first // BANK][:, first % BANK : first % BANK + width],
+                scalar=mean_var_i[:, 0:1],
+                in1=gain_i[:, first : first + width],
                 op0=ALU.subtract,
                 op1=ALU.mult,
             )
+
+        def finish(first, width, func):
+            cols = slice(first, first + width)
             nc.vector.scalar_tensor_tensor(
                 out=g_sum[:, cols],
-                in0=centred_h[:, cols],
-                scalar=rstd_h[:],
-                in1=i_part[:, cols],
+                in0=centred_i[:, cols],
+                scalar=rstd_i[:],
+                in1=h_part[:, cols],
                 op0=ALU.mult,
                 op1=ALU.add,
             )
             nc.scalar.activation(out=gate[:, cols], in_=g_sum[:, cols], func=func)
+
         gate_in = gate[:, 0:CELL]
         gate_forget = gate[:, CELL : 2 * CELL]
         gate_cell = gate[:, 2 * CELL : 3 * CELL]
         gate_out = gate[:, 3 * CELL : 4 * CELL]
 
+        centre(0, 2 * CELL)
+        centre(2 * CELL, CELL)
+        finish(0, 2 * CELL, ACT.Sigmoid)
+        finish(2 * CELL, CELL, ACT.Tanh)
+
         kept = keep.tile([P, CELL], F32)
         nc.vector.tensor_mul(out=kept[:], in0=gate_forget, in1=ac_sb[:])
+        centre(3 * CELL, CELL)
+        finish(3 * CELL, CELL, ACT.Sigmoid)
         fresh = keep.tile([P, CELL], F32)
         nc.vector.tensor_mul(out=fresh[:], in0=gate_in, in1=gate_cell)
         cell = keep.tile([P, CELL], F32)
@@ -297,7 +304,7 @@ def tile_adaptivelstmcell_pa_s_kernel(
             out=centred_c[:],
             in0=cell[:],
             scalar=mean_var_c[:, 0:1],
-            in1=gain_c,
+            in1=gain_c[:],
             op0=ALU.subtract,
             op1=ALU.mult,
         )
@@ -306,7 +313,7 @@ def tile_adaptivelstmcell_pa_s_kernel(
             out=acy[:],
             in0=centred_c[:],
             scalar=rstd_c[:],
-            in1=shift_c,
+            in1=shift_c[:],
             op0=ALU.mult,
             op1=ALU.add,
         )

@@ -65,19 +65,6 @@ def tile_adaptivelstmcell_pa_s_kernel(
             gates = slice(2 * pair, 2 * pair + 2)
             nc.sync.dma_start(out=whh_sb[:, gates, :], in_=whh_rows[:, gates, :])
 
-        ln_rows = keep.tile([P, CELL], BF16)
-        nc.vector.memset(ln_rows[:], 0.0)
-        ROW_SHIFT_I, ROW_SHIFT_H, ROW_GAIN_H, LN_ROWS = 0, 4, 8, 12
-        for first_row, vector in (
-            (ROW_SHIFT_I, a_ln_i_b),
-            (ROW_SHIFT_H, a_ln_h_b),
-            (ROW_GAIN_H, a_ln_h_w),
-        ):
-            nc.sync.dma_start(
-                out=ln_rows[first_row : first_row + GATES, :],
-                in_=vector.rearrange("(r c) -> r c", c=CELL),
-            )
-
         ai_sb = keep.tile([P, K_IH], BF16)
         nc.sync.dma_start(out=ai_sb[:, 0:X_FEATURES], in_=x)
         nc.sync.dma_start(out=ai_sb[:, X_FEATURES:K_IH], in_=hx)
@@ -88,22 +75,18 @@ def tile_adaptivelstmcell_pa_s_kernel(
 
         ac_sb = keep.tile([P, CELL], BF16)
         nc.sync.dma_start(out=ac_sb[:], in_=ac)
+        gain_h = keep.tile([P, N], BF16)
+        nc.sync.dma_start(out=gain_h[:], in_=a_ln_h_w.partition_broadcast(P))
+        shift_i = keep.tile([P, N], BF16)
+        nc.sync.dma_start(out=shift_i[:], in_=a_ln_i_b.partition_broadcast(P))
+        shift_h = keep.tile([P, N], BF16)
+        nc.sync.dma_start(out=shift_h[:], in_=a_ln_h_b.partition_broadcast(P))
         gain_i = keep.tile([P, N], BF16)
         nc.sync.dma_start(out=gain_i[:], in_=a_ln_i_w.partition_broadcast(P))
         gain_c = keep.tile([P, CELL], BF16)
         nc.sync.dma_start(out=gain_c[:], in_=a_ln_c_w.partition_broadcast(P))
         shift_c = keep.tile([P, CELL], BF16)
         nc.sync.dma_start(out=shift_c[:], in_=a_ln_c_b.partition_broadcast(P))
-
-        def spread(columns, first, name):
-            bank = banks.tile([P, 4 * P], F32, tag="bank", name=name)
-            for i in range(4):
-                nc.tensor.transpose(
-                    bank[:, i * P : (i + 1) * P],
-                    columns[:, first + i : first + i + 1].to_broadcast([P, P]),
-                    ident_f32[:],
-                )
-            return bank
 
         def inverse_std(mean_var, name):
             shifted = keep.tile([P, 1], F32, name=name + "_var_eps")
@@ -133,19 +116,6 @@ def tile_adaptivelstmcell_pa_s_kernel(
                 in_=whh_bank[:].rearrange("p (g r) j -> p g j r", g=2, r=2),
             )
 
-        ln_bank = banks.tile([P, P], F32, tag="bank")
-        nc.tensor.transpose(ln_bank[:], ln_rows[:].bitcast(F32), ident_f32[:])
-        ln_columns = keep.tile([P, LN_ROWS], F32)
-        nc.vector.tensor_copy(out=ln_columns[:], in_=ln_bank[:, 0:LN_ROWS])
-        ln_values = ln_columns[:].bitcast(BF16)
-        shift_columns = keep.tile([P, 2 * GATES], F32)
-        nc.vector.tensor_tensor(
-            out=shift_columns[:],
-            in0=ln_values[:, 2 * ROW_SHIFT_I : 2 * ROW_SHIFT_I + 2 * GATES],
-            in1=ln_values[:, 2 * ROW_SHIFT_H : 2 * ROW_SHIFT_H + 2 * GATES],
-            op=ALU.add,
-        )
-
         whhT_values = whhT[:].bitcast(BF16).rearrange("p (n e) -> p n e", e=2)
         vh = [sums.tile([P, BANK], F32, name="vh%d" % half) for half in range(HALVES)]
         stats_h = keep.tile([P, HALVES, 6], F32)
@@ -163,18 +133,8 @@ def tile_adaptivelstmcell_pa_s_kernel(
         nc.vector.bn_aggr(out=mean_var_h[:], in_=stats_h[:].rearrange("p c s -> p (c s)"))
         rstd_h = inverse_std(mean_var_h, "rstd_h")
 
-        gain_h = keep.tile([P, BANK], F32)
-        nc.scalar.copy(out=gain_h[:], in_=spread(ln_columns, ROW_GAIN_H, "gain_h_ps")[:])
         shift_sum = keep.tile([P, N], F32)
-        for half in range(HALVES):
-            nc.scalar.copy(
-                out=shift_sum[:, half * BANK : (half + 1) * BANK].rearrange(
-                    "p (r w e) -> p r w e", r=2, e=2
-                ),
-                in_=spread(shift_columns, 4 * half, "shift_ps%d" % half)[:].rearrange(
-                    "p (r e w) -> p r w e", r=2, e=2
-                ),
-            )
+        nc.vector.tensor_tensor(out=shift_sum[:], in0=shift_i[:], in1=shift_h[:], op=ALU.add)
 
         centred_h = keep.tile([P, N], F32)
         for half in range(HALVES):
@@ -183,7 +143,7 @@ def tile_adaptivelstmcell_pa_s_kernel(
                 out=centred_h[:, cols],
                 in0=vh[half][:],
                 scalar=mean_var_h[:, 0:1],
-                in1=gain_h[:].bitcast(BF16)[:, cols],
+                in1=gain_h[:, cols],
                 op0=ALU.subtract,
                 op1=ALU.mult,
             )

@@ -65,6 +65,19 @@ def tile_adaptivelstmcell_pa_s_kernel(
             gates = slice(2 * pair, 2 * pair + 2)
             nc.sync.dma_start(out=whh_sb[:, gates, :], in_=whh_rows[:, gates, :])
 
+        ln_rows = keep.tile([P, CELL], BF16)
+        nc.vector.memset(ln_rows[:], 0.0)
+        ROW_SHIFT_I, ROW_SHIFT_H, ROW_GAIN_H, LN_ROWS = 0, 4, 8, 12
+        for first_row, vector in (
+            (ROW_SHIFT_I, a_ln_i_b),
+            (ROW_SHIFT_H, a_ln_h_b),
+            (ROW_GAIN_H, a_ln_h_w),
+        ):
+            nc.sync.dma_start(
+                out=ln_rows[first_row : first_row + GATES, :],
+                in_=vector.rearrange("(r c) -> r c", c=CELL),
+            )
+
         ai_sb = keep.tile([P, K_IH], BF16)
         nc.sync.dma_start(out=ai_sb[:, 0:X_FEATURES], in_=x)
         nc.sync.dma_start(out=ai_sb[:, X_FEATURES:K_IH], in_=hx)
@@ -73,20 +86,24 @@ def tile_adaptivelstmcell_pa_s_kernel(
         for g in range(GATES):
             nc.sync.dma_start(out=wih_sb[:, g, :], in_=wih_rows[:, g, :])
 
-        ac_sb = keep.tile([P, CELL], BF16)
-        nc.sync.dma_start(out=ac_sb[:], in_=ac)
-        gain_h = keep.tile([P, N], BF16)
-        nc.sync.dma_start(out=gain_h[:], in_=a_ln_h_w.partition_broadcast(P))
-        shift_i = keep.tile([P, N], BF16)
-        nc.sync.dma_start(out=shift_i[:], in_=a_ln_i_b.partition_broadcast(P))
-        shift_h = keep.tile([P, N], BF16)
-        nc.sync.dma_start(out=shift_h[:], in_=a_ln_h_b.partition_broadcast(P))
         gain_i = keep.tile([P, N], BF16)
         nc.sync.dma_start(out=gain_i[:], in_=a_ln_i_w.partition_broadcast(P))
+        ac_sb = keep.tile([P, CELL], BF16)
+        nc.sync.dma_start(out=ac_sb[:], in_=ac)
         gain_c = keep.tile([P, CELL], BF16)
         nc.sync.dma_start(out=gain_c[:], in_=a_ln_c_w.partition_broadcast(P))
         shift_c = keep.tile([P, CELL], BF16)
         nc.sync.dma_start(out=shift_c[:], in_=a_ln_c_b.partition_broadcast(P))
+
+        def spread(columns, first, name):
+            bank = banks.tile([P, 4 * P], F32, tag="bank", name=name)
+            for i in range(4):
+                nc.tensor.transpose(
+                    bank[:, i * P : (i + 1) * P],
+                    columns[:, first + i : first + i + 1].to_broadcast([P, P]),
+                    ident_f32[:],
+                )
+            return bank
 
         def inverse_std(mean_var, name):
             shifted = keep.tile([P, 1], F32, name=name + "_var_eps")
@@ -98,7 +115,7 @@ def tile_adaptivelstmcell_pa_s_kernel(
         ah_bank = banks.tile([P, P], F32, tag="bank")
         nc.tensor.transpose(ah_bank[:], ah_sb[:].bitcast(F32), ident_f32[:])
         ahT = keep.tile([P, 2, P], BF16)
-        nc.vector.tensor_copy(
+        nc.scalar.copy(
             out=ahT[:], in_=ah_bank[:].bitcast(BF16).rearrange("p (b e) -> p e b", e=2)
         )
         whhT = keep.tile([P, N], F32)
@@ -109,12 +126,24 @@ def tile_adaptivelstmcell_pa_s_kernel(
                 nc.tensor.transpose(
                     whh_bank[:, gr, :], words[:, (gr % 2) * P : (gr % 2 + 1) * P], ident_f32[:]
                 )
-            nc.vector.tensor_copy(
+            nc.scalar.copy(
                 out=whhT[:, pair * BANK : (pair + 1) * BANK].rearrange(
                     "p (g j r) -> p g j r", g=2, r=2
                 ),
                 in_=whh_bank[:].rearrange("p (g r) j -> p g j r", g=2, r=2),
             )
+        ln_bank = banks.tile([P, P], F32, tag="bank")
+        nc.tensor.transpose(ln_bank[:], ln_rows[:].bitcast(F32), ident_f32[:])
+        ln_columns = keep.tile([P, LN_ROWS], F32)
+        nc.vector.tensor_copy(out=ln_columns[:], in_=ln_bank[:, 0:LN_ROWS])
+        ln_values = ln_columns[:].bitcast(BF16)
+        shift_columns = keep.tile([P, 2 * GATES], F32)
+        nc.vector.tensor_tensor(
+            out=shift_columns[:],
+            in0=ln_values[:, 2 * ROW_SHIFT_I : 2 * ROW_SHIFT_I + 2 * GATES],
+            in1=ln_values[:, 2 * ROW_SHIFT_H : 2 * ROW_SHIFT_H + 2 * GATES],
+            op=ALU.add,
+        )
 
         whhT_values = whhT[:].bitcast(BF16).rearrange("p (n e) -> p n e", e=2)
         vh = [sums.tile([P, BANK], F32, name="vh%d" % half) for half in range(HALVES)]
@@ -132,30 +161,6 @@ def tile_adaptivelstmcell_pa_s_kernel(
         mean_var_h = keep.tile([P, 2], F32)
         nc.vector.bn_aggr(out=mean_var_h[:], in_=stats_h[:].rearrange("p c s -> p (c s)"))
         rstd_h = inverse_std(mean_var_h, "rstd_h")
-
-        shift_sum = keep.tile([P, N], F32)
-        nc.vector.tensor_tensor(out=shift_sum[:], in0=shift_i[:], in1=shift_h[:], op=ALU.add)
-
-        centred_h = keep.tile([P, N], F32)
-        for half in range(HALVES):
-            cols = slice(half * BANK, (half + 1) * BANK)
-            nc.vector.scalar_tensor_tensor(
-                out=centred_h[:, cols],
-                in0=vh[half][:],
-                scalar=mean_var_h[:, 0:1],
-                in1=gain_h[:, cols],
-                op0=ALU.subtract,
-                op1=ALU.mult,
-            )
-        h_part = keep.tile([P, N], F32)
-        nc.vector.scalar_tensor_tensor(
-            out=h_part[:],
-            in0=centred_h[:],
-            scalar=rstd_h[:],
-            in1=shift_sum[:],
-            op0=ALU.mult,
-            op1=ALU.add,
-        )
 
         ai_bank = banks.tile([P, 2, P], F32, tag="bank")
         for u in range(2):
@@ -191,13 +196,13 @@ def tile_adaptivelstmcell_pa_s_kernel(
                 in_=w_grouped[:, g, :].bitcast(BF16),
             )
 
-        vi = [sums.tile([P, BANK], F32, name="vi%d" % half) for half in range(HALVES)]
+        vi_banks = [sums.tile([P, BANK], F32, name="vi%d" % bank) for bank in range(2)]
+        vi = [vi_banks[g % 2][:, (g // 2) * CELL : (g // 2 + 1) * CELL] for g in range(GATES)]
         stats_i = keep.tile([P, GATES, 6], F32)
         for g in range(GATES):
             gate_cols = slice(g * CELL, (g + 1) * CELL)
-            vi_gate = vi[g // 2][:, (g % 2) * CELL : (g % 2 + 1) * CELL]
             nc.tensor.matmul_mx(
-                out=vi_gate,
+                out=vi[g],
                 lhsT=ai_codes[:].bitcast(FP8X4),
                 lhsT_scale=ai_scales[:],
                 rhs=w_codes[:, gate_cols].bitcast(FP8X4),
@@ -205,27 +210,62 @@ def tile_adaptivelstmcell_pa_s_kernel(
                 start=True,
                 stop=True,
             )
-            nc.vector.bn_stats(out=stats_i[:, g, :], in_=vi_gate)
+            nc.vector.bn_stats(out=stats_i[:, g, :], in_=vi[g])
         mean_var_i = keep.tile([P, 2], F32)
         nc.vector.bn_aggr(out=mean_var_i[:], in_=stats_i[:].rearrange("p c s -> p (c s)"))
         rstd_i = inverse_std(mean_var_i, "rstd_i")
 
+        gain_h = keep.tile([P, BANK], F32)
+        nc.scalar.copy(out=gain_h[:], in_=spread(ln_columns, ROW_GAIN_H, "gain_h_ps")[:])
+        shift_sum = keep.tile([P, N], F32)
+        for half in range(HALVES):
+            nc.scalar.copy(
+                out=shift_sum[:, half * BANK : (half + 1) * BANK].rearrange(
+                    "p (r w e) -> p r w e", r=2, e=2
+                ),
+                in_=spread(shift_columns, 4 * half, "shift_ps%d" % half)[:].rearrange(
+                    "p (r e w) -> p r w e", r=2, e=2
+                ),
+            )
+
+        centred_h = keep.tile([P, N], F32)
+        h_part = keep.tile([P, N], F32)
         centred_i = keep.tile([P, N], F32)
         g_sum = keep.tile([P, N], F32)
         gate = keep.tile([P, N], F32)
 
-        def centre(first, width):
+        def add_h(first, width):
+            cols = slice(first, first + width)
             nc.vector.scalar_tensor_tensor(
-                out=centred_i[:, first : first + width],
-                in0=vi[first // BANK][:, first % BANK : first % BANK + width],
+                out=centred_h[:, cols],
+                in0=vh[first // BANK][:, first % BANK : first % BANK + width],
+                scalar=mean_var_h[:, 0:1],
+                in1=gain_h[:].bitcast(BF16)[:, cols],
+                op0=ALU.subtract,
+                op1=ALU.mult,
+            )
+            nc.vector.scalar_tensor_tensor(
+                out=h_part[:, cols],
+                in0=centred_h[:, cols],
+                scalar=rstd_h[:],
+                in1=shift_sum[:, cols],
+                op0=ALU.mult,
+                op1=ALU.add,
+            )
+
+        def centre(g):
+            cols = slice(g * CELL, (g + 1) * CELL)
+            nc.vector.scalar_tensor_tensor(
+                out=centred_i[:, cols],
+                in0=vi[g],
                 scalar=mean_var_i[:, 0:1],
-                in1=gain_i[:, first : first + width],
+                in1=gain_i[:, cols],
                 op0=ALU.subtract,
                 op1=ALU.mult,
             )
 
-        def finish(first, width, func):
-            cols = slice(first, first + width)
+        def finish(g, func):
+            cols = slice(g * CELL, (g + 1) * CELL)
             nc.vector.scalar_tensor_tensor(
                 out=g_sum[:, cols],
                 in0=centred_i[:, cols],
@@ -236,20 +276,25 @@ def tile_adaptivelstmcell_pa_s_kernel(
             )
             nc.scalar.activation(out=gate[:, cols], in_=g_sum[:, cols], func=func)
 
-        gate_in = gate[:, 0:CELL]
-        gate_forget = gate[:, CELL : 2 * CELL]
-        gate_cell = gate[:, 2 * CELL : 3 * CELL]
-        gate_out = gate[:, 3 * CELL : 4 * CELL]
+        IN, FORGET, CELL_GATE, OUT = 0, 1, 2, 3
+        gate_in = gate[:, IN * CELL : (IN + 1) * CELL]
+        gate_forget = gate[:, FORGET * CELL : (FORGET + 1) * CELL]
+        gate_cell = gate[:, CELL_GATE * CELL : (CELL_GATE + 1) * CELL]
+        gate_out = gate[:, OUT * CELL : (OUT + 1) * CELL]
 
-        centre(0, 2 * CELL)
-        centre(2 * CELL, CELL)
-        finish(0, 2 * CELL, ACT.Sigmoid)
-        finish(2 * CELL, CELL, ACT.Tanh)
+        add_h(IN * CELL, 2 * CELL)
+        add_h(CELL_GATE * CELL, CELL)
+        for g in (FORGET, IN, CELL_GATE):
+            centre(g)
+        finish(FORGET, ACT.Sigmoid)
+        finish(IN, ACT.Sigmoid)
+        finish(CELL_GATE, ACT.Tanh)
 
         kept = keep.tile([P, CELL], F32)
         nc.vector.tensor_mul(out=kept[:], in0=gate_forget, in1=ac_sb[:])
-        centre(3 * CELL, CELL)
-        finish(3 * CELL, CELL, ACT.Sigmoid)
+        add_h(OUT * CELL, CELL)
+        centre(OUT)
+        finish(OUT, ACT.Sigmoid)
         fresh = keep.tile([P, CELL], F32)
         nc.vector.tensor_mul(out=fresh[:], in0=gate_in, in1=gate_cell)
         cell = keep.tile([P, CELL], F32)

@@ -61,9 +61,8 @@ def tile_adaptivelstmcell_pa_s_kernel(
         nc.sync.dma_start(out=ah_sb[:], in_=ah)
         whh_sb = keep.tile([P, GATES, 2 * K_HH], BF16)
         whh_rows = a_w_hh.rearrange("(g p r) k -> p g (r k)", g=GATES, p=P, r=2)
-        for pair in range(HALVES):
-            gates = slice(2 * pair, 2 * pair + 2)
-            nc.sync.dma_start(out=whh_sb[:, gates, :], in_=whh_rows[:, gates, :])
+        for g in range(GATES):
+            nc.sync.dma_start(out=whh_sb[:, g, :], in_=whh_rows[:, g, :])
 
         ln_rows = keep.tile([P, CELL], BF16)
         nc.vector.memset(ln_rows[:], 0.0)
@@ -105,6 +104,10 @@ def tile_adaptivelstmcell_pa_s_kernel(
                 )
             return bank
 
+        def gates_in_two_banks(name):
+            two = [sums.tile([P, BANK], F32, name="%s%d" % (name, bank)) for bank in range(2)]
+            return [two[g % 2][:, (g // 2) * CELL : (g // 2 + 1) * CELL] for g in range(GATES)]
+
         def inverse_std(mean_var, name):
             shifted = keep.tile([P, 1], F32, name=name + "_var_eps")
             nc.vector.tensor_scalar_add(out=shifted[:], in0=mean_var[:, 1:2], scalar1=EPS)
@@ -119,19 +122,32 @@ def tile_adaptivelstmcell_pa_s_kernel(
             out=ahT[:], in_=ah_bank[:].bitcast(BF16).rearrange("p (b e) -> p e b", e=2)
         )
         whhT = keep.tile([P, N], F32)
-        for pair in range(HALVES):
-            whh_bank = banks.tile([P, 4, P], F32, tag="bank")
-            for gr in range(4):
-                words = whh_sb[:, 2 * pair + gr // 2, :].bitcast(F32)
-                nc.tensor.transpose(
-                    whh_bank[:, gr, :], words[:, (gr % 2) * P : (gr % 2 + 1) * P], ident_f32[:]
-                )
+        whhT_values = whhT[:].bitcast(BF16).rearrange("p (n e) -> p n e", e=2)
+        vh = gates_in_two_banks("vh")
+        stats_h = keep.tile([P, GATES, 6], F32)
+        for g in range(GATES):
+            gate_cols = slice(g * CELL, (g + 1) * CELL)
+            whh_bank = banks.tile([P, 2, P], F32, tag="bank")
+            words = whh_sb[:, g, :].bitcast(F32)
+            for r in range(2):
+                nc.tensor.transpose(whh_bank[:, r, :], words[:, r * P : (r + 1) * P], ident_f32[:])
             nc.scalar.copy(
-                out=whhT[:, pair * BANK : (pair + 1) * BANK].rearrange(
-                    "p (g j r) -> p g j r", g=2, r=2
-                ),
-                in_=whh_bank[:].rearrange("p (g r) j -> p g j r", g=2, r=2),
+                out=whhT[:, gate_cols].rearrange("p (j r) -> p j r", r=2),
+                in_=whh_bank[:].rearrange("p r j -> p j r"),
             )
+            for e in range(2):
+                nc.tensor.matmul(
+                    out=vh[g],
+                    lhsT=ahT[:, e, :],
+                    rhs=whhT_values[:, gate_cols, e],
+                    start=(e == 0),
+                    stop=(e == 1),
+                )
+            nc.vector.bn_stats(out=stats_h[:, g, :], in_=vh[g])
+        mean_var_h = keep.tile([P, 2], F32)
+        nc.vector.bn_aggr(out=mean_var_h[:], in_=stats_h[:].rearrange("p c s -> p (c s)"))
+        rstd_h = inverse_std(mean_var_h, "rstd_h")
+
         ln_bank = banks.tile([P, P], F32, tag="bank")
         nc.tensor.transpose(ln_bank[:], ln_rows[:].bitcast(F32), ident_f32[:])
         ln_columns = keep.tile([P, LN_ROWS], F32)
@@ -144,23 +160,6 @@ def tile_adaptivelstmcell_pa_s_kernel(
             in1=ln_values[:, 2 * ROW_SHIFT_H : 2 * ROW_SHIFT_H + 2 * GATES],
             op=ALU.add,
         )
-
-        whhT_values = whhT[:].bitcast(BF16).rearrange("p (n e) -> p n e", e=2)
-        vh = [sums.tile([P, BANK], F32, name="vh%d" % half) for half in range(HALVES)]
-        stats_h = keep.tile([P, HALVES, 6], F32)
-        for half in range(HALVES):
-            for e in range(2):
-                nc.tensor.matmul(
-                    out=vh[half][:],
-                    lhsT=ahT[:, e, :],
-                    rhs=whhT_values[:, half * BANK : (half + 1) * BANK, e],
-                    start=(e == 0),
-                    stop=(e == 1),
-                )
-            nc.vector.bn_stats(out=stats_h[:, half, :], in_=vh[half][:])
-        mean_var_h = keep.tile([P, 2], F32)
-        nc.vector.bn_aggr(out=mean_var_h[:], in_=stats_h[:].rearrange("p c s -> p (c s)"))
-        rstd_h = inverse_std(mean_var_h, "rstd_h")
 
         ai_bank = banks.tile([P, 2, P], F32, tag="bank")
         for u in range(2):
@@ -196,8 +195,7 @@ def tile_adaptivelstmcell_pa_s_kernel(
                 in_=w_grouped[:, g, :].bitcast(BF16),
             )
 
-        vi_banks = [sums.tile([P, BANK], F32, name="vi%d" % bank) for bank in range(2)]
-        vi = [vi_banks[g % 2][:, (g // 2) * CELL : (g // 2 + 1) * CELL] for g in range(GATES)]
+        vi = gates_in_two_banks("vi")
         stats_i = keep.tile([P, GATES, 6], F32)
         for g in range(GATES):
             gate_cols = slice(g * CELL, (g + 1) * CELL)
@@ -234,11 +232,11 @@ def tile_adaptivelstmcell_pa_s_kernel(
         g_sum = keep.tile([P, N], F32)
         gate = keep.tile([P, N], F32)
 
-        def add_h(first, width):
-            cols = slice(first, first + width)
+        def add_h(g):
+            cols = slice(g * CELL, (g + 1) * CELL)
             nc.vector.scalar_tensor_tensor(
                 out=centred_h[:, cols],
-                in0=vh[first // BANK][:, first % BANK : first % BANK + width],
+                in0=vh[g],
                 scalar=mean_var_h[:, 0:1],
                 in1=gain_h[:].bitcast(BF16)[:, cols],
                 op0=ALU.subtract,
@@ -282,8 +280,8 @@ def tile_adaptivelstmcell_pa_s_kernel(
         gate_cell = gate[:, CELL_GATE * CELL : (CELL_GATE + 1) * CELL]
         gate_out = gate[:, OUT * CELL : (OUT + 1) * CELL]
 
-        add_h(IN * CELL, 2 * CELL)
-        add_h(CELL_GATE * CELL, CELL)
+        for g in (FORGET, IN, CELL_GATE):
+            add_h(g)
         for g in (FORGET, IN, CELL_GATE):
             centre(g)
         finish(FORGET, ACT.Sigmoid)
@@ -292,7 +290,7 @@ def tile_adaptivelstmcell_pa_s_kernel(
 
         kept = keep.tile([P, CELL], F32)
         nc.vector.tensor_mul(out=kept[:], in0=gate_forget, in1=ac_sb[:])
-        add_h(OUT * CELL, CELL)
+        add_h(OUT)
         centre(OUT)
         finish(OUT, ACT.Sigmoid)
         fresh = keep.tile([P, CELL], F32)

@@ -57,13 +57,6 @@ def tile_adaptivelstmcell_pa_s_kernel(
         nc.vector.memset(warm_in[:], 0.0)
         nc.scalar.activation(out=warm_out[:], in_=warm_in[:], func=ACT.Sigmoid)
 
-        ah_sb = keep.tile([P, K_HH], BF16)
-        nc.sync.dma_start(out=ah_sb[:], in_=ah)
-        whh_sb = keep.tile([P, GATES, 2 * K_HH], BF16)
-        whh_rows = a_w_hh.rearrange("(g p r) k -> p g (r k)", g=GATES, p=P, r=2)
-        for g in range(GATES):
-            nc.sync.dma_start(out=whh_sb[:, g, :], in_=whh_rows[:, g, :])
-
         ln_rows = keep.tile([P, CELL], BF16)
         nc.vector.memset(ln_rows[:], 0.0)
         ROW_SHIFT_I, ROW_SHIFT_H, ROW_GAIN_H, LN_ROWS = 0, 4, 8, 12
@@ -72,10 +65,17 @@ def tile_adaptivelstmcell_pa_s_kernel(
             (ROW_SHIFT_H, a_ln_h_b),
             (ROW_GAIN_H, a_ln_h_w),
         ):
-            nc.sync.dma_start(
+            nc.gpsimd.dma_start(
                 out=ln_rows[first_row : first_row + GATES, :],
                 in_=vector.rearrange("(r c) -> r c", c=CELL),
             )
+
+        ah_sb = keep.tile([P, K_HH], BF16)
+        nc.sync.dma_start(out=ah_sb[:], in_=ah)
+        whh_sb = keep.tile([P, GATES, 2 * K_HH], BF16)
+        whh_rows = a_w_hh.rearrange("(g p r) k -> p g (r k)", g=GATES, p=P, r=2)
+        for g in range(GATES):
+            nc.sync.dma_start(out=whh_sb[:, g, :], in_=whh_rows[:, g, :])
 
         ai_sb = keep.tile([P, K_IH], BF16)
         nc.sync.dma_start(out=ai_sb[:, 0:X_FEATURES], in_=x)
@@ -108,12 +108,13 @@ def tile_adaptivelstmcell_pa_s_kernel(
             two = [sums.tile([P, BANK], F32, name="%s%d" % (name, bank)) for bank in range(2)]
             return [two[g % 2][:, (g // 2) * CELL : (g // 2 + 1) * CELL] for g in range(GATES)]
 
-        def inverse_std(mean_var, name):
-            shifted = keep.tile([P, 1], F32, name=name + "_var_eps")
-            nc.vector.tensor_scalar_add(out=shifted[:], in0=mean_var[:, 1:2], scalar1=EPS)
-            rstd = keep.tile([P, 1], F32, name=name)
-            nc.gpsimd.tensor_tensor(out=rstd[:], in0=shifted[:], in1=minus_half[:], op=ALU.pow)
-            return rstd
+        def mean_and_inverse_std(stats, count, name):
+            nc.vector.tensor_scalar_add(out=stats[:, 0, 2:3], in0=stats[:, 0, 2:3], scalar1=EPS * count)
+            mean_var = keep.tile([P, 2], F32, name=name + "_mean_var")
+            nc.vector.bn_aggr(out=mean_var[:], in_=stats[:].rearrange("p c s -> p (c s)"))
+            rstd = keep.tile([P, 1], F32, name=name + "_rstd")
+            nc.gpsimd.tensor_tensor(out=rstd[:], in0=mean_var[:, 1:2], in1=minus_half[:], op=ALU.pow)
+            return mean_var[:, 0:1], rstd[:]
 
         ah_bank = banks.tile([P, P], F32, tag="bank")
         nc.tensor.transpose(ah_bank[:], ah_sb[:].bitcast(F32), ident_f32[:])
@@ -144,9 +145,7 @@ def tile_adaptivelstmcell_pa_s_kernel(
                     stop=(e == 1),
                 )
             nc.vector.bn_stats(out=stats_h[:, g, :], in_=vh[g])
-        mean_var_h = keep.tile([P, 2], F32)
-        nc.vector.bn_aggr(out=mean_var_h[:], in_=stats_h[:].rearrange("p c s -> p (c s)"))
-        rstd_h = inverse_std(mean_var_h, "rstd_h")
+        mean_h, rstd_h = mean_and_inverse_std(stats_h, N, "h")
 
         ln_bank = banks.tile([P, P], F32, tag="bank")
         nc.tensor.transpose(ln_bank[:], ln_rows[:].bitcast(F32), ident_f32[:])
@@ -209,22 +208,11 @@ def tile_adaptivelstmcell_pa_s_kernel(
                 stop=True,
             )
             nc.vector.bn_stats(out=stats_i[:, g, :], in_=vi[g])
-        mean_var_i = keep.tile([P, 2], F32)
-        nc.vector.bn_aggr(out=mean_var_i[:], in_=stats_i[:].rearrange("p c s -> p (c s)"))
-        rstd_i = inverse_std(mean_var_i, "rstd_i")
+        mean_i, rstd_i = mean_and_inverse_std(stats_i, N, "i")
 
         gain_h = keep.tile([P, BANK], F32)
         nc.scalar.copy(out=gain_h[:], in_=spread(ln_columns, ROW_GAIN_H, "gain_h_ps")[:])
-        shift_sum = keep.tile([P, N], F32)
-        for half in range(HALVES):
-            nc.scalar.copy(
-                out=shift_sum[:, half * BANK : (half + 1) * BANK].rearrange(
-                    "p (r w e) -> p r w e", r=2, e=2
-                ),
-                in_=spread(shift_columns, 4 * half, "shift_ps%d" % half)[:].rearrange(
-                    "p (r e w) -> p r w e", r=2, e=2
-                ),
-            )
+        shift_banks = [spread(shift_columns, 4 * half, "shift_ps%d" % half) for half in range(HALVES)]
 
         centred_h = keep.tile([P, N], F32)
         h_part = keep.tile([P, N], F32)
@@ -232,21 +220,25 @@ def tile_adaptivelstmcell_pa_s_kernel(
         g_sum = keep.tile([P, N], F32)
         gate = keep.tile([P, N], F32)
 
-        def add_h(g):
+        def centre_h(g):
             cols = slice(g * CELL, (g + 1) * CELL)
             nc.vector.scalar_tensor_tensor(
                 out=centred_h[:, cols],
                 in0=vh[g],
-                scalar=mean_var_h[:, 0:1],
+                scalar=mean_h,
                 in1=gain_h[:].bitcast(BF16)[:, cols],
                 op0=ALU.subtract,
                 op1=ALU.mult,
             )
+
+        def scale_h(g):
+            cols = slice(g * CELL, (g + 1) * CELL)
+            shift_of_gate = shift_banks[g // 2][:, (g % 2) * CELL : (g % 2 + 1) * CELL]
             nc.vector.scalar_tensor_tensor(
-                out=h_part[:, cols],
-                in0=centred_h[:, cols],
-                scalar=rstd_h[:],
-                in1=shift_sum[:, cols],
+                out=h_part[:, cols].rearrange("p (w e) -> p w e", e=2),
+                in0=centred_h[:, cols].rearrange("p (w e) -> p w e", e=2),
+                scalar=rstd_h,
+                in1=shift_of_gate.rearrange("p (e w) -> p w e", e=2),
                 op0=ALU.mult,
                 op1=ALU.add,
             )
@@ -256,7 +248,7 @@ def tile_adaptivelstmcell_pa_s_kernel(
             nc.vector.scalar_tensor_tensor(
                 out=centred_i[:, cols],
                 in0=vi[g],
-                scalar=mean_var_i[:, 0:1],
+                scalar=mean_i,
                 in1=gain_i[:, cols],
                 op0=ALU.subtract,
                 op1=ALU.mult,
@@ -267,7 +259,7 @@ def tile_adaptivelstmcell_pa_s_kernel(
             nc.vector.scalar_tensor_tensor(
                 out=g_sum[:, cols],
                 in0=centred_i[:, cols],
-                scalar=rstd_i[:],
+                scalar=rstd_i,
                 in1=h_part[:, cols],
                 op0=ALU.mult,
                 op1=ALU.add,
@@ -281,7 +273,9 @@ def tile_adaptivelstmcell_pa_s_kernel(
         gate_out = gate[:, OUT * CELL : (OUT + 1) * CELL]
 
         for g in (FORGET, IN, CELL_GATE):
-            add_h(g)
+            centre_h(g)
+        for g in (FORGET, IN, CELL_GATE):
+            scale_h(g)
         for g in (FORGET, IN, CELL_GATE):
             centre(g)
         finish(FORGET, ACT.Sigmoid)
@@ -290,40 +284,47 @@ def tile_adaptivelstmcell_pa_s_kernel(
 
         kept = keep.tile([P, CELL], F32)
         nc.vector.tensor_mul(out=kept[:], in0=gate_forget, in1=ac_sb[:])
-        add_h(OUT)
+        centre_h(OUT)
         centre(OUT)
+        scale_h(OUT)
         finish(OUT, ACT.Sigmoid)
+        halves = [slice(half * CELL // 2, (half + 1) * CELL // 2) for half in range(2)]
         fresh = keep.tile([P, CELL], F32)
-        nc.vector.tensor_mul(out=fresh[:], in0=gate_in, in1=gate_cell)
         cell = keep.tile([P, CELL], F32)
-        nc.vector.tensor_add(out=cell[:], in0=kept[:], in1=fresh[:])
-        stats_c = keep.tile([P, 6], F32)
-        nc.vector.bn_stats(out=stats_c[:], in_=cell[:])
-        mean_var_c = keep.tile([P, 2], F32)
-        nc.vector.bn_aggr(out=mean_var_c[:], in_=stats_c[:])
-        rstd_c = inverse_std(mean_var_c, "rstd_c")
+        stats_c = keep.tile([P, 2, 6], F32)
+        for cols in halves:
+            nc.vector.tensor_mul(out=fresh[:, cols], in0=gate_in[:, cols], in1=gate_cell[:, cols])
+        for cols in halves:
+            nc.vector.tensor_add(out=cell[:, cols], in0=kept[:, cols], in1=fresh[:, cols])
+        for half, cols in enumerate(halves):
+            nc.vector.bn_stats(out=stats_c[:, half, :], in_=cell[:, cols])
+        mean_c, rstd_c = mean_and_inverse_std(stats_c, CELL, "c")
         centred_c = keep.tile([P, CELL], F32)
-        nc.vector.scalar_tensor_tensor(
-            out=centred_c[:],
-            in0=cell[:],
-            scalar=mean_var_c[:, 0:1],
-            in1=gain_c[:],
-            op0=ALU.subtract,
-            op1=ALU.mult,
-        )
+        for cols in halves:
+            nc.vector.scalar_tensor_tensor(
+                out=centred_c[:, cols],
+                in0=cell[:, cols],
+                scalar=mean_c,
+                in1=gain_c[:, cols],
+                op0=ALU.subtract,
+                op1=ALU.mult,
+            )
         acy = keep.tile([P, CELL], F32)
-        nc.vector.scalar_tensor_tensor(
-            out=acy[:],
-            in0=centred_c[:],
-            scalar=rstd_c[:],
-            in1=shift_c[:],
-            op0=ALU.mult,
-            op1=ALU.add,
-        )
+        for cols in halves:
+            nc.vector.scalar_tensor_tensor(
+                out=acy[:, cols],
+                in0=centred_c[:, cols],
+                scalar=rstd_c,
+                in1=shift_c[:, cols],
+                op0=ALU.mult,
+                op1=ALU.add,
+            )
         nc.sync.dma_start(out=out_1, in_=acy[:])
 
         tanh_acy = keep.tile([P, CELL], F32)
-        nc.scalar.activation(out=tanh_acy[:], in_=acy[:], func=ACT.Tanh)
         ada = keep.tile([P, CELL], F32)
-        nc.vector.tensor_mul(out=ada[:], in0=gate_out, in1=tanh_acy[:])
+        for cols in halves:
+            nc.scalar.activation(out=tanh_acy[:, cols], in_=acy[:, cols], func=ACT.Tanh)
+        for cols in halves:
+            nc.vector.tensor_mul(out=ada[:, cols], in0=gate_out[:, cols], in1=tanh_acy[:, cols])
         nc.sync.dma_start(out=out_0, in_=ada[:])

@@ -57,6 +57,13 @@ def tile_adaptivelstmcell_pa_s_kernel(
         nc.vector.memset(warm_in[:], 0.0)
         nc.scalar.activation(out=warm_out[:], in_=warm_in[:], func=ACT.Sigmoid)
 
+        ah_sb = keep.tile([P, K_HH], BF16)
+        nc.sync.dma_start(out=ah_sb[:], in_=ah)
+        whh_sb = keep.tile([P, GATES, 2 * K_HH], BF16)
+        whh_rows = a_w_hh.rearrange("(g p r) k -> p g (r k)", g=GATES, p=P, r=2)
+        for g in range(GATES):
+            nc.sync.dma_start(out=whh_sb[:, g, :], in_=whh_rows[:, g, :])
+
         ln_rows = keep.tile([P, CELL], BF16)
         nc.vector.memset(ln_rows[:], 0.0)
         ROW_SHIFT_I, ROW_SHIFT_H, ROW_GAIN_H, LN_ROWS = 0, 4, 8, 12
@@ -65,17 +72,10 @@ def tile_adaptivelstmcell_pa_s_kernel(
             (ROW_SHIFT_H, a_ln_h_b),
             (ROW_GAIN_H, a_ln_h_w),
         ):
-            nc.gpsimd.dma_start(
+            nc.sync.dma_start(
                 out=ln_rows[first_row : first_row + GATES, :],
                 in_=vector.rearrange("(r c) -> r c", c=CELL),
             )
-
-        ah_sb = keep.tile([P, K_HH], BF16)
-        nc.sync.dma_start(out=ah_sb[:], in_=ah)
-        whh_sb = keep.tile([P, GATES, 2 * K_HH], BF16)
-        whh_rows = a_w_hh.rearrange("(g p r) k -> p g (r k)", g=GATES, p=P, r=2)
-        for g in range(GATES):
-            nc.sync.dma_start(out=whh_sb[:, g, :], in_=whh_rows[:, g, :])
 
         ai_sb = keep.tile([P, K_IH], BF16)
         nc.sync.dma_start(out=ai_sb[:, 0:X_FEATURES], in_=x)

from contextlib import ExitStack

import concourse.mybir as mybir
from concourse.masks import make_identity

F32 = mybir.dt.float32
BF16 = mybir.dt.bfloat16
U32 = mybir.dt.uint32
U8 = mybir.dt.uint8
FP8X4 = mybir.dt.float8_e4m3fn_x4
ALU = mybir.AluOpType
ACT = mybir.ActivationFunctionType

P = 128
X_FEATURES = 128
K_IH = 512
K_HH = 256
CELL = 256
GATES = 4
N = GATES * CELL
BANK = 512
HALVES = N // BANK
EPS = 1e-5

FLOPS = 2 * P * N * (K_IH + K_HH)


def tile_adaptivelstmcell_pa_s_kernel(
    tc,
    x,
    hx,
    ah,
    ac,
    a_w_ih,
    a_w_hh,
    a_ln_i_w,
    a_ln_i_b,
    a_ln_h_w,
    a_ln_h_b,
    a_ln_c_w,
    a_ln_c_b,
    out_0,
    out_1,
):
    nc = tc.nc
    with ExitStack() as ctx:
        keep = ctx.enter_context(tc.tile_pool(name="keep", bufs=1))
        banks = ctx.enter_context(tc.psum_pool(name="banks", bufs=4))
        sums = ctx.enter_context(tc.psum_pool(name="sums", bufs=1))

        ident_f32 = keep.tile([P, P], F32)
        make_identity(nc, ident_f32[:])
        minus_half = keep.tile([P, 1], F32)
        nc.vector.memset(minus_half[:], -0.5)
        warm_in = keep.tile([P, 1], F32)
        warm_out = keep.tile([P, 1], F32)
        nc.vector.memset(warm_in[:], 0.0)
        nc.scalar.activation(out=warm_out[:], in_=warm_in[:], func=ACT.Sigmoid)

        ah_sb = keep.tile([P, K_HH], BF16)
        nc.sync.dma_start(out=ah_sb[:], in_=ah)
        whh_sb = keep.tile([P, GATES, 2 * K_HH], BF16)
        whh_rows = a_w_hh.rearrange("(g p r) k -> p g (r k)", g=GATES, p=P, r=2)
        for g in range(GATES):
            nc.sync.dma_start(out=whh_sb[:, g, :], in_=whh_rows[:, g, :])

        ln_rows = keep.tile([P, CELL], BF16)
        nc.vector.memset(ln_rows[:], 0.0)
        ROW_SHIFT_I, ROW_SHIFT_H, ROW_GAIN_H, LN_ROWS = 0, 4, 8, 12
        for first_row, vector in (
            (ROW_SHIFT_I, a_ln_i_b),
            (ROW_SHIFT_H, a_ln_h_b),
            (ROW_GAIN_H, a_ln_h_w),
        ):
            nc.sync.dma_start(
                out=ln_rows[first_row : first_row + GATES, :],
                in_=vector.rearrange("(r c) -> r c", c=CELL),
            )

        ai_sb = keep.tile([P, K_IH], BF16)
        nc.sync.dma_start(out=ai_sb[:, 0:X_FEATURES], in_=x)
        nc.sync.dma_start(out=ai_sb[:, X_FEATURES:K_IH], in_=hx)
        wih_sb = keep.tile([P, GATES, 2 * K_IH], BF16)
        wih_rows = a_w_ih.rearrange("(g p r) k -> p g (r k)", g=GATES, p=P, r=2)
        for g in range(GATES):
            nc.sync.dma_start(out=wih_sb[:, g, :], in_=wih_rows[:, g, :])

        gain_i = keep.tile([P, N], BF16)
        nc.sync.dma_start(out=gain_i[:], in_=a_ln_i_w.partition_broadcast(P))
        ac_sb = keep.tile([P, CELL], BF16)
        nc.sync.dma_start(out=ac_sb[:], in_=ac)
        gain_c = keep.tile([P, CELL], BF16)
        nc.sync.dma_start(out=gain_c[:], in_=a_ln_c_w.partition_broadcast(P))
        shift_c = keep.tile([P, CELL], BF16)
        nc.sync.dma_start(out=shift_c[:], in_=a_ln_c_b.partition_broadcast(P))

        def spread(columns, first, name):
            bank = banks.tile([P, 4 * P], F32, tag="bank", name=name)
            for i in range(4):
                nc.tensor.transpose(
                    bank[:, i * P : (i + 1) * P],
                    columns[:, first + i : first + i + 1].to_broadcast([P, P]),
                    ident_f32[:],
                )
            return bank

        def gates_in_two_banks(name):
            two = [sums.tile([P, BANK], F32, name="%s%d" % (name, bank)) for bank in range(2)]
            return [two[g % 2][:, (g // 2) * CELL : (g // 2 + 1) * CELL] for g in range(GATES)]

        def mean_and_inverse_std(stats, count, name):
            nc.vector.tensor_scalar_add(out=stats[:, 0, 2:3], in0=stats[:, 0, 2:3], scalar1=EPS * count)
            mean_var = keep.tile([P, 2], F32, name=name + "_mean_var")
            nc.vector.bn_aggr(out=mean_var[:], in_=stats[:].rearrange("p c s -> p (c s)"))
            rstd = keep.tile([P, 1], F32, name=name + "_rstd")
            nc.gpsimd.tensor_tensor(out=rstd[:], in0=mean_var[:, 1:2], in1=minus_half[:], op=ALU.pow)
            return mean_var[:, 0:1], rstd[:]

        ah_bank = banks.tile([P, P], F32, tag="bank")
        nc.tensor.transpose(ah_bank[:], ah_sb[:].bitcast(F32), ident_f32[:])
        ahT = keep.tile([P, 2, P], BF16)
        nc.scalar.copy(
            out=ahT[:], in_=ah_bank[:].bitcast(BF16).rearrange("p (b e) -> p e b", e=2)
        )
        whhT = keep.tile([P, N], F32)
        whhT_values = whhT[:].bitcast(BF16).rearrange("p (n e) -> p n e", e=2)
        vh = gates_in_two_banks("vh")
        stats_h = keep.tile([P, GATES, 6], F32)
        for g in range(GATES):
            gate_cols = slice(g * CELL, (g + 1) * CELL)
            whh_bank = banks.tile([P, 2, P], F32, tag="bank")
            words = whh_sb[:, g, :].bitcast(F32)
            for r in range(2):
                nc.tensor.transpose(whh_bank[:, r, :], words[:, r * P : (r + 1) * P], ident_f32[:])
            nc.scalar.copy(
                out=whhT[:, gate_cols].rearrange("p (j r) -> p j r", r=2),
                in_=whh_bank[:].rearrange("p r j -> p j r"),
            )
            for e in range(2):
                nc.tensor.matmul(
                    out=vh[g],
                    lhsT=ahT[:, e, :],
                    rhs=whhT_values[:, gate_cols, e],
                    start=(e == 0),
                    stop=(e == 1),
                )
            nc.vector.bn_stats(out=stats_h[:, g, :], in_=vh[g])
        mean_h, rstd_h = mean_and_inverse_std(stats_h, N, "h")

        ln_bank = banks.tile([P, P], F32, tag="bank")
        nc.tensor.transpose(ln_bank[:], ln_rows[:].bitcast(F32), ident_f32[:])
        ln_columns = keep.tile([P, LN_ROWS], F32)
        nc.vector.tensor_copy(out=ln_columns[:], in_=ln_bank[:, 0:LN_ROWS])
        ln_values = ln_columns[:].bitcast(BF16)
        shift_columns = keep.tile([P, 2 * GATES], F32)
        nc.vector.tensor_tensor(
            out=shift_columns[:],
            in0=ln_values[:, 2 * ROW_SHIFT_I : 2 * ROW_SHIFT_I + 2 * GATES],
            in1=ln_values[:, 2 * ROW_SHIFT_H : 2 * ROW_SHIFT_H + 2 * GATES],
            op=ALU.add,
        )

        ai_bank = banks.tile([P, 2, P], F32, tag="bank")
        for u in range(2):
            nc.tensor.transpose(
                ai_bank[:, u, :], ai_sb[:].bitcast(F32)[:, u * P : (u + 1) * P], ident_f32[:]
            )
        ai_grouped = keep.tile([P, P, 2], F32, align_bytes=64)
        nc.scalar.copy(out=ai_grouped[:], in_=ai_bank[:].rearrange("p u b -> p b u"))
        ai_codes = keep.tile([P, P], U32, align_bytes=64)
        ai_scales = keep.tile([P, P], U8, align_bytes=64)
        nc.vector.quantize_mx(
            out=ai_codes[:].bitcast(FP8X4),
            scales=ai_scales[:],
            in_=ai_grouped[:].rearrange("p b u -> p (b u)").bitcast(BF16),
        )

        w_grouped = keep.tile([P, GATES, 2 * CELL], F32, align_bytes=64)
        w_codes = keep.tile([P, N], U32, align_bytes=64)
        w_scales = keep.tile([P, N], U8, align_bytes=64)
        for g in range(GATES):
            w_bank = banks.tile([P, 4, P], F32, tag="bank")
            words = wih_sb[:, g, :].bitcast(F32)
            for ru in range(4):
                nc.tensor.transpose(w_bank[:, ru, :], words[:, ru * P : (ru + 1) * P], ident_f32[:])
            nc.scalar.copy(
                out=w_grouped[:, g, :].rearrange("p (j r u) -> p j r u", r=2, u=2),
                in_=w_bank[:].rearrange("p (r u) j -> p j r u", r=2, u=2),
            )
            gate_cols = slice(g * CELL, (g + 1) * CELL)
            nc.vector.quantize_mx(
                out=w_codes[:, gate_cols].bitcast(FP8X4),
                scales=w_scales[:, gate_cols],
                in_=w_grouped[:, g, :].bitcast(BF16),
            )

        vi = gates_in_two_banks("vi")
        stats_i = keep.tile([P, GATES, 6], F32)
        for g in range(GATES):
            gate_cols = slice(g * CELL, (g + 1) * CELL)
            nc.tensor.matmul_mx(
                out=vi[g],
                lhsT=ai_codes[:].bitcast(FP8X4),
                lhsT_scale=ai_scales[:],
                rhs=w_codes[:, gate_cols].bitcast(FP8X4),
                rhs_scale=w_scales[:, gate_cols],
                start=True,
                stop=True,
            )
            nc.vector.bn_stats(out=stats_i[:, g, :], in_=vi[g])
        mean_i, rstd_i = mean_and_inverse_std(stats_i, N, "i")

        gain_h = keep.tile([P, BANK], F32)
        nc.scalar.copy(out=gain_h[:], in_=spread(ln_columns, ROW_GAIN_H, "gain_h_ps")[:])
        shift_banks = [spread(shift_columns, 4 * half, "shift_ps%d" % half) for half in range(HALVES)]

        centred_h = keep.tile([P, N], F32)
        h_part = keep.tile([P, N], F32)
        centred_i = keep.tile([P, N], F32)
        g_sum = keep.tile([P, N], F32)
        gate = keep.tile([P, N], F32)

        def centre_h(g):
            cols = slice(g * CELL, (g + 1) * CELL)
            nc.vector.scalar_tensor_tensor(
                out=centred_h[:, cols],
                in0=vh[g],
                scalar=mean_h,
                in1=gain_h[:].bitcast(BF16)[:, cols],
                op0=ALU.subtract,
                op1=ALU.mult,
            )

        def scale_h(g):
            cols = slice(g * CELL, (g + 1) * CELL)
            shift_of_gate = shift_banks[g // 2][:, (g % 2) * CELL : (g % 2 + 1) * CELL]
            nc.vector.scalar_tensor_tensor(
                out=h_part[:, cols].rearrange("p (w e) -> p w e", e=2),
                in0=centred_h[:, cols].rearrange("p (w e) -> p w e", e=2),
                scalar=rstd_h,
                in1=shift_of_gate.rearrange("p (e w) -> p w e", e=2),
                op0=ALU.mult,
                op1=ALU.add,
            )

        def centre(g):
            cols = slice(g * CELL, (g + 1) * CELL)
            nc.vector.scalar_tensor_tensor(
                out=centred_i[:, cols],
                in0=vi[g],
                scalar=mean_i,
                in1=gain_i[:, cols],
                op0=ALU.subtract,
                op1=ALU.mult,
            )

        def finish(g, func):
            cols = slice(g * CELL, (g + 1) * CELL)
            nc.vector.scalar_tensor_tensor(
                out=g_sum[:, cols],
                in0=centred_i[:, cols],
                scalar=rstd_i,
                in1=h_part[:, cols],
                op0=ALU.mult,
                op1=ALU.add,
            )
            nc.scalar.activation(out=gate[:, cols], in_=g_sum[:, cols], func=func)

        IN, FORGET, CELL_GATE, OUT = 0, 1, 2, 3
        gate_in = gate[:, IN * CELL : (IN + 1) * CELL]
        gate_forget = gate[:, FORGET * CELL : (FORGET + 1) * CELL]
        gate_cell = gate[:, CELL_GATE * CELL : (CELL_GATE + 1) * CELL]
        gate_out = gate[:, OUT * CELL : (OUT + 1) * CELL]

        for g in (FORGET, IN, CELL_GATE):
            centre_h(g)
        for g in (FORGET, IN, CELL_GATE):
            scale_h(g)
        for g in (FORGET, IN, CELL_GATE):
            centre(g)
        finish(FORGET, ACT.Sigmoid)
        finish(IN, ACT.Sigmoid)
        finish(CELL_GATE, ACT.Tanh)

        kept = keep.tile([P, CELL], F32)
        nc.vector.tensor_mul(out=kept[:], in0=gate_forget, in1=ac_sb[:])
        centre_h(OUT)
        centre(OUT)
        scale_h(OUT)
        finish(OUT, ACT.Sigmoid)
        halves = [slice(half * CELL // 2, (half + 1) * CELL // 2) for half in range(2)]
        fresh = keep.tile([P, CELL], F32)
        cell = keep.tile([P, CELL], F32)
        stats_c = keep.tile([P, 2, 6], F32)
        for cols in halves:
            nc.vector.tensor_mul(out=fresh[:, cols], in0=gate_in[:, cols], in1=gate_cell[:, cols])
        for cols in halves:
            nc.vector.tensor_add(out=cell[:, cols], in0=kept[:, cols], in1=fresh[:, cols])
        for half, cols in enumerate(halves):
            nc.vector.bn_stats(out=stats_c[:, half, :], in_=cell[:, cols])
        mean_c, rstd_c = mean_and_inverse_std(stats_c, CELL, "c")
        centred_c = keep.tile([P, CELL], F32)
        for cols in halves:
            nc.vector.scalar_tensor_tensor(
                out=centred_c[:, cols],
                in0=cell[:, cols],
                scalar=mean_c,
                in1=gain_c[:, cols],
                op0=ALU.subtract,
                op1=ALU.mult,
            )
        acy = keep.tile([P, CELL], F32)
        for cols in halves:
            nc.vector.scalar_tensor_tensor(
                out=acy[:, cols],
                in0=centred_c[:, cols],
                scalar=rstd_c,
                in1=shift_c[:, cols],
                op0=ALU.mult,
                op1=ALU.add,
            )
        nc.sync.dma_start(out=out_1, in_=acy[:])

        tanh_acy = keep.tile([P, CELL], F32)
        ada = keep.tile([P, CELL], F32)
        for cols in halves:
            nc.scalar.activation(out=tanh_acy[:, cols], in_=acy[:, cols], func=ACT.Tanh)
        for cols in halves:
            nc.vector.tensor_mul(out=ada[:, cols], in0=gate_out[:, cols], in1=tanh_acy[:, cols])
        nc.sync.dma_start(out=out_0, in_=ada[:])
